import numpy as np
import ml_dtypes

BF16 = ml_dtypes.bfloat16


def bf(x):
    return np.asarray(x, np.float32).astype(BF16)


def f32(x):
    return np.asarray(x, np.float32)


def f64(x):
    return np.asarray(x).astype(np.float64)


def striped(idx):
    return np.tile(idx.reshape(-1, 16).T, (8, 1))


M, A, C, S, N = 4, 128, 1024, 2048, 1024
DENS, HSTD = 0.03125, 2.0


def setup_inputs():
    x = bf(np.random.standard_normal((M, A, N)))
    adj_t = bf(np.random.uniform(0.0, 1.0, (N, N)) * (np.random.uniform(0.0, 1.0, (N, N)) < DENS))
    weight = bf(np.random.uniform(-1.0, 1.0, (M, A, C)) * HSTD * np.sqrt(3.0 / (M * A)))
    bias = f32(np.random.uniform(0.0, 1.0, (C, 1)))
    base = f32(np.random.standard_normal((C, S)))
    return {"x": x, "adj_t": adj_t, "weight": weight, "bias": bias, "base": base, "offs": striped(np.random.permutation(S)[:N])}


def reference(x, adj_t, weight, bias, base, offs):
    idx = offs[:16].T.reshape(-1)
    h = sum(f64(weight)[m].T @ f64(x)[m] for m in range(M))
    mx_t = f64(adj_t) + np.eye(N)
    d = mx_t.sum(axis=0)
    u = (h @ mx_t) / d[None, :]
    out = f64(base).copy()
    out[:, idx] = np.maximum(u, 0.0) + f64(bias)
    return out

@@ -1,0 +1,117 @@
+import concourse.mybir as mybir
+from concourse.masks import make_identity
+
+BF16, F32, U16 = mybir.dt.bfloat16, mybir.dt.float32, mybir.dt.uint16
+ALU = mybir.AluOpType
+COPY = mybir.ActivationFunctionType.Copy
+IDENTITY = mybir.ActivationFunctionType.Identity
+
+P = 128
+M = 4
+N = 1024
+C = 1024
+S = 2048
+BANK = 512
+NODE_BLOCKS = N // P
+CHANNEL_BLOCKS = C // P
+HALVES = N // BANK
+BLOCKS_PER_BANK = BANK // P
+
+FLOPS = 2 * M * P * C * N + 2 * C * N * N
+
+
+def tile_spconvlayer_b_kernel(tc, x, adj_t, weight, bias, base, offs, out):
+    nc = tc.nc
+    with (
+        tc.tile_pool(name="held", bufs=1) as held,
+        tc.tile_pool(name="work", bufs=2) as work,
+        tc.psum_pool(name="psum", bufs=2) as psum,
+    ):
+        offsets = held.tile([P, N // 16], U16, name="offsets")
+        nc.sync.dma_start(offsets[:], offs)
+
+        neighbours = [held.tile([P, N], BF16, name=f"neighbours{kb}") for kb in range(NODE_BLOCKS)]
+        for kb in range(NODE_BLOCKS):
+            nc.sync.dma_start(neighbours[kb][:], adj_t[kb * P : (kb + 1) * P, :])
+
+        features = held.tile([P, M, N], BF16, name="features")
+        nc.sync.dma_start(features[:], x.rearrange("m a k -> a m k"))
+        weights = held.tile([P, M, C], BF16, name="weights")
+        nc.sync.dma_start(weights[:], weight.rearrange("m a c -> a m c"))
+
+        bias_rows = held.tile([P, P], F32, name="bias_rows")
+        nc.vector.memset(bias_rows[:], 0.0)
+        nc.sync.dma_start(bias_rows[0:CHANNEL_BLOCKS, :], bias.rearrange("(b p) o -> b (p o)", p=P))
+
+        windows = [held.tile([P, S], F32, name=f"window{cb}") for cb in range(CHANNEL_BLOCKS)]
+        for cb in range(CHANNEL_BLOCKS):
+            nc.sync.dma_start(windows[cb][:], base[cb * P : (cb + 1) * P, :])
+
+        identity_f32 = held.tile([P, P], F32, name="identity_f32")
+        make_identity(nc, identity_f32[:])
+        identity_bf16 = held.tile([P, P], BF16, name="identity_bf16")
+        make_identity(nc, identity_bf16[:])
+        ones = held.tile([P, P], BF16, name="ones")
+        nc.vector.memset(ones[:], 1.0)
+
+        inv_degree = held.tile([P, N], F32, name="inv_degree")
+        for half in range(HALVES):
+            cols = slice(half * BANK, (half + 1) * BANK)
+            sums = psum.tile([P, BANK], F32, name="sums", tag="setup")
+            for kb in range(NODE_BLOCKS):
+                nc.tensor.matmul(
+                    sums[:], ones[:], neighbours[kb][:, cols],
+                    start=(kb == 0), stop=(kb == NODE_BLOCKS - 1),
+                )
+            degree = work.tile([P, BANK], F32, name="degree")
+            nc.scalar.activation(degree[:], sums[:], COPY, bias=1.0)
+            nc.vector.reciprocal(inv_degree[:, cols], degree[:])
+
+        for kb in range(NODE_BLOCKS):
+            diagonal = neighbours[kb][:, kb * P : (kb + 1) * P]
+            nc.gpsimd.tensor_tensor(diagonal, diagonal, identity_bf16[:], ALU.add)
+
+        bias_flipped = psum.tile([P, P], F32, name="bias_flipped", tag="setup")
+        nc.tensor.transpose(bias_flipped[:], bias_rows[:], identity_f32[:])
+        bias_cols = held.tile([P, CHANNEL_BLOCKS], F32, name="bias_cols")
+        nc.scalar.copy(bias_cols[:], bias_flipped[:, 0:CHANNEL_BLOCKS])
+        zeros = held.tile([P, N], F32, name="zeros")
+        nc.gpsimd.memset(zeros[:], 0.0)
+
+        for cb in range(CHANNEL_BLOCKS):
+            channels = slice(cb * P, (cb + 1) * P)
+
+            projected = work.tile([P, NODE_BLOCKS, P], BF16, name="projected")
+            for bank in range(NODE_BLOCKS // BLOCKS_PER_BANK):
+                h_sums = psum.tile([P, BLOCKS_PER_BANK, P], F32, name="h_sums")
+                for i in range(BLOCKS_PER_BANK):
+                    kb = bank * BLOCKS_PER_BANK + i
+                    for m in range(M):
+                        nc.tensor.matmul(
+                            h_sums[:, i, :], features[:, m, kb * P : (kb + 1) * P], weights[:, m, channels],
+                            start=(m == 0), stop=(m == M - 1),
+                        )
+                nc.scalar.copy(
+                    projected[:, bank * BLOCKS_PER_BANK : (bank + 1) * BLOCKS_PER_BANK, :], h_sums[:]
+                )
+
+            relu_u = work.tile([P, N], F32, name="relu_u")
+            for half in range(HALVES):
+                cols = slice(half * BANK, (half + 1) * BANK)
+                u_sums = psum.tile([P, BANK], F32, name="u_sums", bufs=4)
+                for kb in range(NODE_BLOCKS):
+                    nc.tensor.matmul(
+                        u_sums[:], projected[:, kb, :], neighbours[kb][:, cols],
+                        start=(kb == 0), stop=(kb == NODE_BLOCKS - 1),
+                    )
+                nc.vector.scalar_tensor_tensor(
+                    relu_u[:, cols], u_sums[:], 0.0, inv_degree[:, cols], ALU.max, ALU.mult
+                )
+
+            bias_wide = work.tile([P, N], F32, name="bias_wide")
+            nc.scalar.activation(bias_wide[:], zeros[:], IDENTITY, bias=bias_cols[:, cb : cb + 1])
+
+            nc.vector.tensor_tensor(
+                windows[cb][:].indirect(offsets[:]), relu_u[:], bias_wide[:], ALU.add
+            )
+            nc.sync.dma_start(out[channels, :], windows[cb][:])

@@ -4,7 +4,6 @@ from concourse.masks import make_identity
 BF16, F32, U16 = mybir.dt.bfloat16, mybir.dt.float32, mybir.dt.uint16
 ALU = mybir.AluOpType
 COPY = mybir.ActivationFunctionType.Copy
-IDENTITY = mybir.ActivationFunctionType.Identity
 
 P = 128
 M = 4
@@ -30,6 +29,10 @@ def tile_spconvlayer_b_kernel(tc, x, adj_t, weight, bias, base, offs, out):
         offsets = held.tile([P, N // 16], U16, name="offsets")
         nc.sync.dma_start(offsets[:], offs)
 
+        bias_rows = held.tile([P, P], F32, name="bias_rows")
+        nc.vector.memset(bias_rows[:], 0.0)
+        nc.sync.dma_start(bias_rows[0:CHANNEL_BLOCKS, :], bias.rearrange("(b p) o -> b (p o)", p=P))
+
         neighbours = [held.tile([P, N], BF16, name=f"neighbours{kb}") for kb in range(NODE_BLOCKS)]
         for kb in range(NODE_BLOCKS):
             nc.sync.dma_start(neighbours[kb][:], adj_t[kb * P : (kb + 1) * P, :])
@@ -38,10 +41,6 @@ def tile_spconvlayer_b_kernel(tc, x, adj_t, weight, bias, base, offs, out):
         nc.sync.dma_start(features[:], x.rearrange("m a k -> a m k"))
         weights = held.tile([P, M, C], BF16, name="weights")
         nc.sync.dma_start(weights[:], weight.rearrange("m a c -> a m c"))
-
-        bias_rows = held.tile([P, P], F32, name="bias_rows")
-        nc.vector.memset(bias_rows[:], 0.0)
-        nc.sync.dma_start(bias_rows[0:CHANNEL_BLOCKS, :], bias.rearrange("(b p) o -> b (p o)", p=P))
 
         windows = [held.tile([P, S], F32, name=f"window{cb}") for cb in range(CHANNEL_BLOCKS)]
         for cb in range(CHANNEL_BLOCKS):
@@ -54,29 +53,29 @@ def tile_spconvlayer_b_kernel(tc, x, adj_t, weight, bias, base, offs, out):
         ones = held.tile([P, P], BF16, name="ones")
         nc.vector.memset(ones[:], 1.0)
 
-        inv_degree = held.tile([P, N], F32, name="inv_degree")
-        for half in range(HALVES):
-            cols = slice(half * BANK, (half + 1) * BANK)
-            sums = psum.tile([P, BANK], F32, name="sums", tag="setup")
-            for kb in range(NODE_BLOCKS):
-                nc.tensor.matmul(
-                    sums[:], ones[:], neighbours[kb][:, cols],
-                    start=(kb == 0), stop=(kb == NODE_BLOCKS - 1),
-                )
-            degree = work.tile([P, BANK], F32, name="degree")
-            nc.scalar.activation(degree[:], sums[:], COPY, bias=1.0)
-            nc.vector.reciprocal(inv_degree[:, cols], degree[:])
-
-        for kb in range(NODE_BLOCKS):
-            diagonal = neighbours[kb][:, kb * P : (kb + 1) * P]
-            nc.gpsimd.tensor_tensor(diagonal, diagonal, identity_bf16[:], ALU.add)
-
         bias_flipped = psum.tile([P, P], F32, name="bias_flipped", tag="setup")
         nc.tensor.transpose(bias_flipped[:], bias_rows[:], identity_f32[:])
         bias_cols = held.tile([P, CHANNEL_BLOCKS], F32, name="bias_cols")
         nc.scalar.copy(bias_cols[:], bias_flipped[:, 0:CHANNEL_BLOCKS])
-        zeros = held.tile([P, N], F32, name="zeros")
-        nc.gpsimd.memset(zeros[:], 0.0)
+        bias_wide = [held.tile([P, N], F32, name=f"bias_wide{cb}") for cb in range(CHANNEL_BLOCKS)]
+        for cb in range(CHANNEL_BLOCKS):
+            nc.gpsimd.tensor_copy(bias_wide[cb][:], bias_cols[:, cb : cb + 1].to_broadcast([P, N]))
+
+        sums = [psum.tile([P, BANK], F32, name=f"sums{half}", tag="setup") for half in range(HALVES)]
+        for kb in range(NODE_BLOCKS):
+            for half in range(HALVES):
+                nc.tensor.matmul(
+                    sums[half][:], ones[:], neighbours[kb][:, half * BANK : (half + 1) * BANK],
+                    start=(kb == 0), stop=(kb == NODE_BLOCKS - 1),
+                )
+            diagonal = neighbours[kb][:, kb * P : (kb + 1) * P]
+            nc.vector.tensor_tensor(diagonal, diagonal, identity_bf16[:], ALU.add)
+
+        inv_degree = held.tile([P, N], F32, name="inv_degree")
+        for half in range(HALVES):
+            degree = work.tile([P, BANK], F32, name="degree")
+            nc.scalar.activation(degree[:], sums[half][:], COPY, bias=1.0)
+            nc.vector.reciprocal(inv_degree[:, half * BANK : (half + 1) * BANK], degree[:])
 
         for cb in range(CHANNEL_BLOCKS):
             channels = slice(cb * P, (cb + 1) * P)
@@ -108,10 +107,7 @@ def tile_spconvlayer_b_kernel(tc, x, adj_t, weight, bias, base, offs, out):
                     relu_u[:, cols], u_sums[:], 0.0, inv_degree[:, cols], ALU.max, ALU.mult
                 )
 
-            bias_wide = work.tile([P, N], F32, name="bias_wide")
-            nc.scalar.activation(bias_wide[:], zeros[:], IDENTITY, bias=bias_cols[:, cb : cb + 1])
-
             nc.vector.tensor_tensor(
-                windows[cb][:].indirect(offsets[:]), relu_u[:], bias_wide[:], ALU.add
+                windows[cb][:].indirect(offsets[:]), relu_u[:], bias_wide[cb][:], ALU.add
             )
             nc.sync.dma_start(out[channels, :], windows[cb][:])

@@ -4,6 +4,7 @@ from concourse.masks import make_identity
 BF16, F32, U16 = mybir.dt.bfloat16, mybir.dt.float32, mybir.dt.uint16
 ALU = mybir.AluOpType
 COPY = mybir.ActivationFunctionType.Copy
+RELU = mybir.ActivationFunctionType.Relu
 
 P = 128
 M = 4
@@ -94,7 +95,7 @@ def tile_spconvlayer_b_kernel(tc, x, adj_t, weight, bias, base, offs, out):
                     projected[:, bank * BLOCKS_PER_BANK : (bank + 1) * BLOCKS_PER_BANK, :], h_sums[:]
                 )
 
-            relu_u = work.tile([P, N], F32, name="relu_u")
+            relu_sums = work.tile([P, N], F32, name="relu_sums")
             for half in range(HALVES):
                 cols = slice(half * BANK, (half + 1) * BANK)
                 u_sums = psum.tile([P, BANK], F32, name="u_sums", bufs=4)
@@ -103,9 +104,9 @@ def tile_spconvlayer_b_kernel(tc, x, adj_t, weight, bias, base, offs, out):
                         u_sums[:], projected[:, kb, :], neighbours[kb][:, cols],
                         start=(kb == 0), stop=(kb == NODE_BLOCKS - 1),
                     )
-                nc.vector.scalar_tensor_tensor(
-                    relu_u[:, cols], u_sums[:], 0.0, inv_degree[:, cols], ALU.max, ALU.mult
-                )
+                nc.scalar.activation(relu_sums[:, cols], u_sums[:], RELU)
+            relu_u = work.tile([P, N], F32, name="relu_u")
+            nc.gpsimd.tensor_tensor(relu_u[:], relu_sums[:], inv_degree[:], ALU.mult)
 
             nc.vector.tensor_tensor(
                 windows[cb][:].indirect(offsets[:]), relu_u[:], bias_wide[cb][:], ALU.add

@@ -4,7 +4,6 @@ from concourse.masks import make_identity
 BF16, F32, U16 = mybir.dt.bfloat16, mybir.dt.float32, mybir.dt.uint16
 ALU = mybir.AluOpType
 COPY = mybir.ActivationFunctionType.Copy
-RELU = mybir.ActivationFunctionType.Relu
 
 P = 128
 M = 4
@@ -30,18 +29,21 @@ def tile_spconvlayer_b_kernel(tc, x, adj_t, weight, bias, base, offs, out):
         offsets = held.tile([P, N // 16], U16, name="offsets")
         nc.sync.dma_start(offsets[:], offs)
 
-        bias_rows = held.tile([P, P], F32, name="bias_rows")
-        nc.vector.memset(bias_rows[:], 0.0)
-        nc.sync.dma_start(bias_rows[0:CHANNEL_BLOCKS, :], bias.rearrange("(b p) o -> b (p o)", p=P))
-
         neighbours = [held.tile([P, N], BF16, name=f"neighbours{kb}") for kb in range(NODE_BLOCKS)]
         for kb in range(NODE_BLOCKS):
             nc.sync.dma_start(neighbours[kb][:], adj_t[kb * P : (kb + 1) * P, :])
 
-        features = held.tile([P, M, N], BF16, name="features")
-        nc.sync.dma_start(features[:], x.rearrange("m a k -> a m k"))
         weights = held.tile([P, M, C], BF16, name="weights")
-        nc.sync.dma_start(weights[:], weight.rearrange("m a c -> a m c"))
+        weight_amc = weight.rearrange("m a c -> a m c")
+        features = held.tile([P, M, N], BF16, name="features")
+        nc.sync.dma_start(weights[:, :, 0:P], weight_amc[:, :, 0:P])
+        nc.sync.dma_start(features[:], x.rearrange("m a k -> a m k"))
+
+        bias_rows = held.tile([P, P], F32, name="bias_rows")
+        nc.vector.memset(bias_rows[:], 0.0)
+        nc.sync.dma_start(bias_rows[0:CHANNEL_BLOCKS, :], bias.rearrange("(b p) o -> b (p o)", p=P))
+
+        nc.sync.dma_start(weights[:, :, P:C], weight_amc[:, :, P:C])
 
         windows = [held.tile([P, S], F32, name=f"window{cb}") for cb in range(CHANNEL_BLOCKS)]
         for cb in range(CHANNEL_BLOCKS):
@@ -53,14 +55,6 @@ def tile_spconvlayer_b_kernel(tc, x, adj_t, weight, bias, base, offs, out):
         make_identity(nc, identity_bf16[:])
         ones = held.tile([P, P], BF16, name="ones")
         nc.vector.memset(ones[:], 1.0)
-
-        bias_flipped = psum.tile([P, P], F32, name="bias_flipped", tag="setup")
-        nc.tensor.transpose(bias_flipped[:], bias_rows[:], identity_f32[:])
-        bias_cols = held.tile([P, CHANNEL_BLOCKS], F32, name="bias_cols")
-        nc.scalar.copy(bias_cols[:], bias_flipped[:, 0:CHANNEL_BLOCKS])
-        bias_wide = [held.tile([P, N], F32, name=f"bias_wide{cb}") for cb in range(CHANNEL_BLOCKS)]
-        for cb in range(CHANNEL_BLOCKS):
-            nc.gpsimd.tensor_copy(bias_wide[cb][:], bias_cols[:, cb : cb + 1].to_broadcast([P, N]))
 
         sums = [psum.tile([P, BANK], F32, name=f"sums{half}", tag="setup") for half in range(HALVES)]
         for kb in range(NODE_BLOCKS):
@@ -77,6 +71,11 @@ def tile_spconvlayer_b_kernel(tc, x, adj_t, weight, bias, base, offs, out):
             degree = work.tile([P, BANK], F32, name="degree")
             nc.scalar.activation(degree[:], sums[half][:], COPY, bias=1.0)
             nc.vector.reciprocal(inv_degree[:, half * BANK : (half + 1) * BANK], degree[:])
+
+        bias_flipped = psum.tile([P, P], F32, name="bias_flipped", tag="setup")
+        nc.tensor.transpose(bias_flipped[:], bias_rows[:], identity_f32[:])
+        bias_cols = held.tile([P, CHANNEL_BLOCKS], F32, name="bias_cols")
+        nc.scalar.copy(bias_cols[:], bias_flipped[:, 0:CHANNEL_BLOCKS])
 
         for cb in range(CHANNEL_BLOCKS):
             channels = slice(cb * P, (cb + 1) * P)
@@ -95,7 +94,7 @@ def tile_spconvlayer_b_kernel(tc, x, adj_t, weight, bias, base, offs, out):
                     projected[:, bank * BLOCKS_PER_BANK : (bank + 1) * BLOCKS_PER_BANK, :], h_sums[:]
                 )
 
-            relu_sums = work.tile([P, N], F32, name="relu_sums")
+            relu_u = work.tile([P, N], F32, name="relu_u")
             for half in range(HALVES):
                 cols = slice(half * BANK, (half + 1) * BANK)
                 u_sums = psum.tile([P, BANK], F32, name="u_sums", bufs=4)
@@ -104,11 +103,14 @@ def tile_spconvlayer_b_kernel(tc, x, adj_t, weight, bias, base, offs, out):
                         u_sums[:], projected[:, kb, :], neighbours[kb][:, cols],
                         start=(kb == 0), stop=(kb == NODE_BLOCKS - 1),
                     )
-                nc.scalar.activation(relu_sums[:, cols], u_sums[:], RELU)
-            relu_u = work.tile([P, N], F32, name="relu_u")
-            nc.gpsimd.tensor_tensor(relu_u[:], relu_sums[:], inv_degree[:], ALU.mult)
+                nc.vector.scalar_tensor_tensor(
+                    relu_u[:, cols], u_sums[:], 0.0, inv_degree[:, cols], ALU.max, ALU.mult
+                )
+
+            bias_wide = held.tile([P, N], F32, name=f"bias_wide{cb}")
+            nc.scalar.copy(bias_wide[:], bias_cols[:, cb : cb + 1].to_broadcast([P, N]))
 
             nc.vector.tensor_tensor(
-                windows[cb][:].indirect(offsets[:]), relu_u[:], bias_wide[cb][:], ALU.add
+                windows[cb][:].indirect(offsets[:]), relu_u[:], bias_wide[:], ALU.add
             )
             nc.sync.dma_start(out[channels, :], windows[cb][:])

@@ -3,7 +3,7 @@ from concourse.masks import make_identity
 
 BF16, F32, U16 = mybir.dt.bfloat16, mybir.dt.float32, mybir.dt.uint16
 ALU = mybir.AluOpType
-COPY = mybir.ActivationFunctionType.Copy
+RELU = mybir.ActivationFunctionType.Relu
 
 P = 128
 M = 4
@@ -29,88 +29,114 @@ def tile_spconvlayer_b_kernel(tc, x, adj_t, weight, bias, base, offs, out):
         offsets = held.tile([P, N // 16], U16, name="offsets")
         nc.sync.dma_start(offsets[:], offs)
 
-        neighbours = [held.tile([P, N], BF16, name=f"neighbours{kb}") for kb in range(NODE_BLOCKS)]
-        for kb in range(NODE_BLOCKS):
-            nc.sync.dma_start(neighbours[kb][:], adj_t[kb * P : (kb + 1) * P, :])
+        bias_cols = held.tile([P, CHANNEL_BLOCKS], F32, name="bias_cols")
+        nc.scalar.dma_start(bias_cols[:], bias.rearrange("(b p) o -> p (b o)", p=P))
 
         weights = held.tile([P, M, C], BF16, name="weights")
         weight_amc = weight.rearrange("m a c -> a m c")
         features = held.tile([P, M, N], BF16, name="features")
-        nc.sync.dma_start(weights[:, :, 0:P], weight_amc[:, :, 0:P])
-        nc.sync.dma_start(features[:], x.rearrange("m a k -> a m k"))
+        x_amk = x.rearrange("m a k -> a m k")
+        nc.sync.dma_start(weights[:, :, 0 : C // 2], weight_amc[:, :, 0 : C // 2])
+        for half in range(HALVES):
+            cols = slice(half * BANK, (half + 1) * BANK)
+            nc.sync.dma_start(features[:, :, cols], x_amk[:, :, cols])
 
-        bias_rows = held.tile([P, P], F32, name="bias_rows")
-        nc.vector.memset(bias_rows[:], 0.0)
-        nc.sync.dma_start(bias_rows[0:CHANNEL_BLOCKS, :], bias.rearrange("(b p) o -> b (p o)", p=P))
-
-        nc.sync.dma_start(weights[:, :, P:C], weight_amc[:, :, P:C])
+        neighbours = [held.tile([P, NODE_BLOCKS, BANK], BF16, name=f"neighbours{half}") for half in range(HALVES)]
+        for half in range(HALVES):
+            cols = slice(half * BANK, (half + 1) * BANK)
+            nc.sync.dma_start(neighbours[half][:], adj_t[:, cols].rearrange("(kb p) j -> p kb j", p=P))
 
         windows = [held.tile([P, S], F32, name=f"window{cb}") for cb in range(CHANNEL_BLOCKS)]
-        for cb in range(CHANNEL_BLOCKS):
+        nc.sync.dma_start(windows[0][:], base[0:P, :])
+        nc.sync.dma_start(weights[:, :, C // 2 : C], weight_amc[:, :, C // 2 : C])
+        for cb in range(1, CHANNEL_BLOCKS):
             nc.sync.dma_start(windows[cb][:], base[cb * P : (cb + 1) * P, :])
 
         identity_f32 = held.tile([P, P], F32, name="identity_f32")
         make_identity(nc, identity_f32[:])
         identity_bf16 = held.tile([P, P], BF16, name="identity_bf16")
         make_identity(nc, identity_bf16[:])
-        ones = held.tile([P, P], BF16, name="ones")
+        ones = held.tile([P, 1], BF16, name="ones")
         nc.vector.memset(ones[:], 1.0)
 
-        sums = [psum.tile([P, BANK], F32, name=f"sums{half}", tag="setup") for half in range(HALVES)]
-        for kb in range(NODE_BLOCKS):
-            for half in range(HALVES):
-                nc.tensor.matmul(
-                    sums[half][:], ones[:], neighbours[kb][:, half * BANK : (half + 1) * BANK],
-                    start=(kb == 0), stop=(kb == NODE_BLOCKS - 1),
-                )
-            diagonal = neighbours[kb][:, kb * P : (kb + 1) * P]
-            nc.vector.tensor_tensor(diagonal, diagonal, identity_bf16[:], ALU.add)
-
-        inv_degree = held.tile([P, N], F32, name="inv_degree")
-        for half in range(HALVES):
-            degree = work.tile([P, BANK], F32, name="degree")
-            nc.scalar.activation(degree[:], sums[half][:], COPY, bias=1.0)
-            nc.vector.reciprocal(inv_degree[:, half * BANK : (half + 1) * BANK], degree[:])
-
-        bias_flipped = psum.tile([P, P], F32, name="bias_flipped", tag="setup")
-        nc.tensor.transpose(bias_flipped[:], bias_rows[:], identity_f32[:])
-        bias_cols = held.tile([P, CHANNEL_BLOCKS], F32, name="bias_cols")
-        nc.scalar.copy(bias_cols[:], bias_flipped[:, 0:CHANNEL_BLOCKS])
-
+        bias_wide = [held.tile([P, N], F32, name=f"bias_wide{cb}") for cb in range(CHANNEL_BLOCKS)]
         for cb in range(CHANNEL_BLOCKS):
-            channels = slice(cb * P, (cb + 1) * P)
+            nc.vector.tensor_copy(bias_wide[cb][:], bias_cols[:, cb : cb + 1].to_broadcast([P, N]))
 
+        def received(kb, jb):
+            first = (jb % BLOCKS_PER_BANK) * P
+            return neighbours[jb // BLOCKS_PER_BANK][:, kb, first : first + P]
+
+        def project(cb):
             projected = work.tile([P, NODE_BLOCKS, P], BF16, name="projected")
-            for bank in range(NODE_BLOCKS // BLOCKS_PER_BANK):
+            for bank in range(HALVES):
                 h_sums = psum.tile([P, BLOCKS_PER_BANK, P], F32, name="h_sums")
                 for i in range(BLOCKS_PER_BANK):
                     kb = bank * BLOCKS_PER_BANK + i
                     for m in range(M):
                         nc.tensor.matmul(
-                            h_sums[:, i, :], features[:, m, kb * P : (kb + 1) * P], weights[:, m, channels],
+                            h_sums[:, i, :], features[:, m, kb * P : (kb + 1) * P],
+                            weights[:, m, cb * P : (cb + 1) * P],
                             start=(m == 0), stop=(m == M - 1),
                         )
                 nc.scalar.copy(
                     projected[:, bank * BLOCKS_PER_BANK : (bank + 1) * BLOCKS_PER_BANK, :], h_sums[:]
                 )
+            return projected
 
-            relu_u = work.tile([P, N], F32, name="relu_u")
-            for half in range(HALVES):
-                cols = slice(half * BANK, (half + 1) * BANK)
-                u_sums = psum.tile([P, BANK], F32, name="u_sums", bufs=4)
-                for kb in range(NODE_BLOCKS):
-                    nc.tensor.matmul(
-                        u_sums[:], projected[:, kb, :], neighbours[kb][:, cols],
-                        start=(kb == 0), stop=(kb == NODE_BLOCKS - 1),
+        def aggregate(projected):
+            averaged = work.tile([P, NODE_BLOCKS, P], F32, name="averaged")
+            for bank in range(HALVES):
+                u_sums = psum.tile([P, BLOCKS_PER_BANK, P], F32, name="u_sums")
+                for i in range(BLOCKS_PER_BANK):
+                    jb = bank * BLOCKS_PER_BANK + i
+                    for kb in range(NODE_BLOCKS):
+                        nc.tensor.matmul(
+                            u_sums[:, i, :],
+                            with_self[:, jb, :] if kb == jb else received(kb, jb),
+                            projected[:, kb, :],
+                            start=(kb == 0), stop=(kb == NODE_BLOCKS - 1),
+                        )
+                for i in range(BLOCKS_PER_BANK):
+                    jb = bank * BLOCKS_PER_BANK + i
+                    nc.scalar.activation(
+                        averaged[:, jb, :], u_sums[:, i, :], RELU, scale=inv_degree[:, jb : jb + 1]
                     )
-                nc.vector.scalar_tensor_tensor(
-                    relu_u[:, cols], u_sums[:], 0.0, inv_degree[:, cols], ALU.max, ALU.mult
-                )
+            return averaged
 
-            bias_wide = held.tile([P, N], F32, name=f"bias_wide{cb}")
-            nc.scalar.copy(bias_wide[:], bias_cols[:, cb : cb + 1].to_broadcast([P, N]))
-
+        def place(cb, averaged):
+            relu_u = work.tile([P, N], F32, name="relu_u")
+            for bank in range(HALVES):
+                flipped = psum.tile([P, BANK], F32, name="flipped")
+                for i in range(BLOCKS_PER_BANK):
+                    jb = bank * BLOCKS_PER_BANK + i
+                    nc.tensor.transpose(flipped[:, i * P : (i + 1) * P], averaged[:, jb, :], identity_f32[:])
+                nc.scalar.copy(relu_u[:, bank * BANK : (bank + 1) * BANK], flipped[:])
             nc.vector.tensor_tensor(
-                windows[cb][:].indirect(offsets[:]), relu_u[:], bias_wide[:], ALU.add
+                windows[cb][:].indirect(offsets[:]), relu_u[:], bias_wide[cb][:], ALU.add
             )
-            nc.sync.dma_start(out[channels, :], windows[cb][:])
+            nc.sync.dma_start(out[cb * P : (cb + 1) * P, :], windows[cb][:])
+
+        projected = project(0)
+
+        with_self = held.tile([P, NODE_BLOCKS, P], BF16, name="with_self")
+        for jb in range(NODE_BLOCKS):
+            nc.vector.tensor_tensor(with_self[:, jb, :], received(jb, jb), identity_bf16[:], ALU.add)
+
+        degree_sums = psum.tile([P, NODE_BLOCKS], F32, name="degree_sums", bufs=1)
+        for jb in range(NODE_BLOCKS):
+            for kb in range(NODE_BLOCKS):
+                nc.tensor.matmul(
+                    degree_sums[:, jb : jb + 1], received(kb, jb), ones[:],
+                    start=(kb == 0), stop=(kb == NODE_BLOCKS - 1),
+                )
+        degree = held.tile([P, NODE_BLOCKS], F32, name="degree")
+        nc.vector.tensor_scalar_add(degree[:], degree_sums[:], 1.0)
+        inv_degree = held.tile([P, NODE_BLOCKS], F32, name="inv_degree")
+        nc.vector.reciprocal(inv_degree[:], degree[:])
+
+        for cb in range(CHANNEL_BLOCKS):
+            averaged = aggregate(projected)
+            if cb + 1 < CHANNEL_BLOCKS:
+                projected = project(cb + 1)
+            place(cb, averaged)

@@ -29,16 +29,13 @@ def tile_spconvlayer_b_kernel(tc, x, adj_t, weight, bias, base, offs, out):
         offsets = held.tile([P, N // 16], U16, name="offsets")
         nc.sync.dma_start(offsets[:], offs)
 
-        bias_cols = held.tile([P, CHANNEL_BLOCKS], F32, name="bias_cols")
-        nc.scalar.dma_start(bias_cols[:], bias.rearrange("(b p) o -> p (b o)", p=P))
-
         weights = held.tile([P, M, C], BF16, name="weights")
         weight_amc = weight.rearrange("m a c -> a m c")
         features = held.tile([P, M, N], BF16, name="features")
         x_amk = x.rearrange("m a k -> a m k")
-        nc.sync.dma_start(weights[:, :, 0 : C // 2], weight_amc[:, :, 0 : C // 2])
-        for half in range(HALVES):
-            cols = slice(half * BANK, (half + 1) * BANK)
+        nc.sync.dma_start(weights[:, :, 0:P], weight_amc[:, :, 0:P])
+        for quarter in range(4):
+            cols = slice(quarter * (N // 4), (quarter + 1) * (N // 4))
             nc.sync.dma_start(features[:, :, cols], x_amk[:, :, cols])
 
         neighbours = [held.tile([P, NODE_BLOCKS, BANK], BF16, name=f"neighbours{half}") for half in range(HALVES)]
@@ -46,10 +43,13 @@ def tile_spconvlayer_b_kernel(tc, x, adj_t, weight, bias, base, offs, out):
             cols = slice(half * BANK, (half + 1) * BANK)
             nc.sync.dma_start(neighbours[half][:], adj_t[:, cols].rearrange("(kb p) j -> p kb j", p=P))
 
+        bias_cols = held.tile([P, CHANNEL_BLOCKS], F32, name="bias_cols")
+        nc.sync.dma_start(bias_cols[:], bias.rearrange("(b p) o -> p (b o)", p=P))
+
+        nc.sync.dma_start(weights[:, :, P:C], weight_amc[:, :, P:C])
+
         windows = [held.tile([P, S], F32, name=f"window{cb}") for cb in range(CHANNEL_BLOCKS)]
-        nc.sync.dma_start(windows[0][:], base[0:P, :])
-        nc.sync.dma_start(weights[:, :, C // 2 : C], weight_amc[:, :, C // 2 : C])
-        for cb in range(1, CHANNEL_BLOCKS):
+        for cb in range(CHANNEL_BLOCKS):
             nc.sync.dma_start(windows[cb][:], base[cb * P : (cb + 1) * P, :])
 
         identity_f32 = held.tile([P, P], F32, name="identity_f32")
@@ -58,10 +58,6 @@ def tile_spconvlayer_b_kernel(tc, x, adj_t, weight, bias, base, offs, out):
         make_identity(nc, identity_bf16[:])
         ones = held.tile([P, 1], BF16, name="ones")
         nc.vector.memset(ones[:], 1.0)
-
-        bias_wide = [held.tile([P, N], F32, name=f"bias_wide{cb}") for cb in range(CHANNEL_BLOCKS)]
-        for cb in range(CHANNEL_BLOCKS):
-            nc.vector.tensor_copy(bias_wide[cb][:], bias_cols[:, cb : cb + 1].to_broadcast([P, N]))
 
         def received(kb, jb):
             first = (jb % BLOCKS_PER_BANK) * P
@@ -134,6 +130,10 @@ def tile_spconvlayer_b_kernel(tc, x, adj_t, weight, bias, base, offs, out):
         nc.vector.tensor_scalar_add(degree[:], degree_sums[:], 1.0)
         inv_degree = held.tile([P, NODE_BLOCKS], F32, name="inv_degree")
         nc.vector.reciprocal(inv_degree[:], degree[:])
+
+        bias_wide = [held.tile([P, N], F32, name=f"bias_wide{cb}") for cb in range(CHANNEL_BLOCKS)]
+        for cb in range(CHANNEL_BLOCKS):
+            nc.vector.tensor_copy(bias_wide[cb][:], bias_cols[:, cb : cb + 1].to_broadcast([P, N]))
 
         for cb in range(CHANNEL_BLOCKS):
             averaged = aggregate(projected)

@@ -80,17 +80,15 @@ def tile_spconvlayer_b_kernel(tc, x, adj_t, weight, bias, base, offs, out):
                 )
             return projected
 
-        def aggregate(projected):
+        def average_nodes_first(projected):
             averaged = work.tile([P, NODE_BLOCKS, P], F32, name="averaged")
             for bank in range(HALVES):
-                u_sums = psum.tile([P, BLOCKS_PER_BANK, P], F32, name="u_sums")
+                u_sums = psum.tile([P, BLOCKS_PER_BANK, P], F32, name="u_sums", bufs=4)
                 for i in range(BLOCKS_PER_BANK):
                     jb = bank * BLOCKS_PER_BANK + i
                     for kb in range(NODE_BLOCKS):
                         nc.tensor.matmul(
-                            u_sums[:, i, :],
-                            with_self[:, jb, :] if kb == jb else received(kb, jb),
-                            projected[:, kb, :],
+                            u_sums[:, i, :], received(kb, jb), projected[:, kb, :],
                             start=(kb == 0), stop=(kb == NODE_BLOCKS - 1),
                         )
                 for i in range(BLOCKS_PER_BANK):
@@ -100,32 +98,38 @@ def tile_spconvlayer_b_kernel(tc, x, adj_t, weight, bias, base, offs, out):
                     )
             return averaged
 
-        def place(cb, averaged):
-            relu_u = work.tile([P, N], F32, name="relu_u")
+        def flip(nodes_first, channels_first):
             for bank in range(HALVES):
                 flipped = psum.tile([P, BANK], F32, name="flipped")
                 for i in range(BLOCKS_PER_BANK):
                     jb = bank * BLOCKS_PER_BANK + i
-                    nc.tensor.transpose(flipped[:, i * P : (i + 1) * P], averaged[:, jb, :], identity_f32[:])
-                nc.scalar.copy(relu_u[:, bank * BANK : (bank + 1) * BANK], flipped[:])
-            nc.vector.tensor_tensor(
-                windows[cb][:].indirect(offsets[:]), relu_u[:], bias_wide[cb][:], ALU.add
-            )
-            nc.sync.dma_start(out[cb * P : (cb + 1) * P, :], windows[cb][:])
+                    nc.tensor.transpose(flipped[:, i * P : (i + 1) * P], nodes_first[:, jb, :], identity_f32[:])
+                nc.scalar.copy(channels_first[:, bank * BANK : (bank + 1) * BANK], flipped[:])
+
+        def average_channels_first(projected, relu_u):
+            for half in range(HALVES):
+                cols = slice(half * BANK, (half + 1) * BANK)
+                u_sums = psum.tile([P, BANK], F32, name="u_sums", bufs=4)
+                for kb in range(NODE_BLOCKS):
+                    nc.tensor.matmul(
+                        u_sums[:], projected[:, kb, :], neighbours[half][:, kb, :],
+                        start=(kb == 0), stop=(kb == NODE_BLOCKS - 1),
+                    )
+                nc.vector.scalar_tensor_tensor(
+                    relu_u[:, cols], u_sums[:], 0.0, inv_degree_row[:, cols], ALU.max, ALU.mult
+                )
 
         projected = project(0)
 
-        with_self = held.tile([P, NODE_BLOCKS, P], BF16, name="with_self")
-        for jb in range(NODE_BLOCKS):
-            nc.vector.tensor_tensor(with_self[:, jb, :], received(jb, jb), identity_bf16[:], ALU.add)
-
-        degree_sums = psum.tile([P, NODE_BLOCKS], F32, name="degree_sums", bufs=1)
+        degree_sums = psum.tile([P, NODE_BLOCKS], F32, name="degree_sums", tag="flipped")
         for jb in range(NODE_BLOCKS):
             for kb in range(NODE_BLOCKS):
                 nc.tensor.matmul(
                     degree_sums[:, jb : jb + 1], received(kb, jb), ones[:],
                     start=(kb == 0), stop=(kb == NODE_BLOCKS - 1),
                 )
+            nc.vector.tensor_tensor(received(jb, jb), received(jb, jb), identity_bf16[:], ALU.add)
+
         degree = held.tile([P, NODE_BLOCKS], F32, name="degree")
         nc.vector.tensor_scalar_add(degree[:], degree_sums[:], 1.0)
         inv_degree = held.tile([P, NODE_BLOCKS], F32, name="inv_degree")
@@ -135,8 +139,24 @@ def tile_spconvlayer_b_kernel(tc, x, adj_t, weight, bias, base, offs, out):
         for cb in range(CHANNEL_BLOCKS):
             nc.vector.tensor_copy(bias_wide[cb][:], bias_cols[:, cb : cb + 1].to_broadcast([P, N]))
 
+        inv_degree_spread = held.tile([P, NODE_BLOCKS, P], F32, name="inv_degree_spread")
+        nc.scalar.copy(inv_degree_spread[:], inv_degree[:].unsqueeze(2).to_broadcast([P, NODE_BLOCKS, P]))
+        inv_degree_row = held.tile([P, N], F32, name="inv_degree_row")
+        flip(inv_degree_spread, inv_degree_row)
+
         for cb in range(CHANNEL_BLOCKS):
-            averaged = aggregate(projected)
+            relu_u = work.tile([P, N], F32, name="relu_u", bufs=3)
+            nodes_first = cb >= CHANNEL_BLOCKS // 2
+            if nodes_first:
+                averaged = average_nodes_first(projected)
+            else:
+                average_channels_first(projected, relu_u)
             if cb + 1 < CHANNEL_BLOCKS:
                 projected = project(cb + 1)
-            place(cb, averaged)
+            if nodes_first:
+                flip(averaged, relu_u)
+
+            nc.vector.tensor_tensor(
+                windows[cb][:].indirect(offsets[:]), relu_u[:], bias_wide[cb][:], ALU.add
+            )
+            nc.sync.dma_start(out[cb * P : (cb + 1) * P, :], windows[cb][:])

@@ -15,6 +15,7 @@ NODE_BLOCKS = N // P
 CHANNEL_BLOCKS = C // P
 HALVES = N // BANK
 BLOCKS_PER_BANK = BANK // P
+CHANNELS_FIRST_BLOCKS = 5
 
 FLOPS = 2 * M * P * C * N + 2 * C * N * N
 
@@ -135,18 +136,22 @@ def tile_spconvlayer_b_kernel(tc, x, adj_t, weight, bias, base, offs, out):
         inv_degree = held.tile([P, NODE_BLOCKS], F32, name="inv_degree")
         nc.vector.reciprocal(inv_degree[:], degree[:])
 
-        bias_wide = [held.tile([P, N], F32, name=f"bias_wide{cb}") for cb in range(CHANNEL_BLOCKS)]
-        for cb in range(CHANNEL_BLOCKS):
-            nc.vector.tensor_copy(bias_wide[cb][:], bias_cols[:, cb : cb + 1].to_broadcast([P, N]))
-
         inv_degree_spread = held.tile([P, NODE_BLOCKS, P], F32, name="inv_degree_spread")
-        nc.scalar.copy(inv_degree_spread[:], inv_degree[:].unsqueeze(2).to_broadcast([P, NODE_BLOCKS, P]))
+        nc.vector.tensor_copy(inv_degree_spread[:], inv_degree[:].unsqueeze(2).to_broadcast([P, NODE_BLOCKS, P]))
         inv_degree_row = held.tile([P, N], F32, name="inv_degree_row")
         flip(inv_degree_spread, inv_degree_row)
 
+        bias_wide = [held.tile([P, N], F32, name=f"bias_wide{cb}") for cb in range(CHANNEL_BLOCKS)]
+        for cb in range(CHANNEL_BLOCKS):
+            repeated = bias_cols[:, cb : cb + 1].to_broadcast([P, N])
+            if cb % 3 == 0:
+                nc.scalar.copy(bias_wide[cb][:], repeated)
+            else:
+                nc.vector.tensor_copy(bias_wide[cb][:], repeated)
+
         for cb in range(CHANNEL_BLOCKS):
             relu_u = work.tile([P, N], F32, name="relu_u", bufs=3)
-            nodes_first = cb >= CHANNEL_BLOCKS // 2
+            nodes_first = cb >= CHANNELS_FIRST_BLOCKS
             if nodes_first:
                 averaged = average_nodes_first(projected)
             else:

@@ -47,10 +47,11 @@ def tile_spconvlayer_b_kernel(tc, x, adj_t, weight, bias, base, offs, out):
         bias_cols = held.tile([P, CHANNEL_BLOCKS], F32, name="bias_cols")
         nc.sync.dma_start(bias_cols[:], bias.rearrange("(b p) o -> p (b o)", p=P))
 
-        nc.sync.dma_start(weights[:, :, P:C], weight_amc[:, :, P:C])
-
         windows = [held.tile([P, S], F32, name=f"window{cb}") for cb in range(CHANNEL_BLOCKS)]
-        for cb in range(CHANNEL_BLOCKS):
+        nc.sync.dma_start(weights[:, :, P : 2 * P], weight_amc[:, :, P : 2 * P])
+        nc.sync.dma_start(windows[0][:], base[0:P, :])
+        nc.sync.dma_start(weights[:, :, 2 * P : C], weight_amc[:, :, 2 * P : C])
+        for cb in range(1, CHANNEL_BLOCKS):
             nc.sync.dma_start(windows[cb][:], base[cb * P : (cb + 1) * P, :])
 
         identity_f32 = held.tile([P, P], F32, name="identity_f32")

@@ -15,7 +15,7 @@ NODE_BLOCKS = N // P
 CHANNEL_BLOCKS = C // P
 HALVES = N // BANK
 BLOCKS_PER_BANK = BANK // P
-CHANNELS_FIRST_BLOCKS = 5
+CHANNELS_FIRST_BLOCKS = 4
 
 FLOPS = 2 * M * P * C * N + 2 * C * N * N
 
@@ -65,22 +65,27 @@ def tile_spconvlayer_b_kernel(tc, x, adj_t, weight, bias, base, offs, out):
             first = (jb % BLOCKS_PER_BANK) * P
             return neighbours[jb // BLOCKS_PER_BANK][:, kb, first : first + P]
 
-        def project(cb):
-            projected = work.tile([P, NODE_BLOCKS, P], BF16, name="projected")
-            for bank in range(HALVES):
-                h_sums = psum.tile([P, BLOCKS_PER_BANK, P], F32, name="h_sums")
-                for i in range(BLOCKS_PER_BANK):
-                    kb = bank * BLOCKS_PER_BANK + i
-                    for m in range(M):
-                        nc.tensor.matmul(
-                            h_sums[:, i, :], features[:, m, kb * P : (kb + 1) * P],
-                            weights[:, m, cb * P : (cb + 1) * P],
-                            start=(m == 0), stop=(m == M - 1),
-                        )
-                nc.scalar.copy(
-                    projected[:, bank * BLOCKS_PER_BANK : (bank + 1) * BLOCKS_PER_BANK, :], h_sums[:]
-                )
-            return projected
+        projected = []
+
+        def project_half():
+            cb, bank = divmod(len(halves_done), HALVES)
+            halves_done.append((cb, bank))
+            if bank == 0:
+                projected.append(work.tile([P, NODE_BLOCKS, P], BF16, name="projected", bufs=3))
+            h_sums = psum.tile([P, BLOCKS_PER_BANK, P], F32, name="h_sums")
+            for i in range(BLOCKS_PER_BANK):
+                kb = bank * BLOCKS_PER_BANK + i
+                for m in range(M):
+                    nc.tensor.matmul(
+                        h_sums[:, i, :], features[:, m, kb * P : (kb + 1) * P],
+                        weights[:, m, cb * P : (cb + 1) * P],
+                        start=(m == 0), stop=(m == M - 1),
+                    )
+            nc.scalar.copy(
+                projected[cb][:, bank * BLOCKS_PER_BANK : (bank + 1) * BLOCKS_PER_BANK, :], h_sums[:]
+            )
+
+        halves_done = []
 
         def average_nodes_first(projected):
             averaged = work.tile([P, NODE_BLOCKS, P], F32, name="averaged")
@@ -121,7 +126,8 @@ def tile_spconvlayer_b_kernel(tc, x, adj_t, weight, bias, base, offs, out):
                     relu_u[:, cols], u_sums[:], 0.0, inv_degree_row[:, cols], ALU.max, ALU.mult
                 )
 
-        projected = project(0)
+        for bank in range(HALVES):
+            project_half()
 
         degree_sums = psum.tile([P, NODE_BLOCKS], F32, name="degree_sums", tag="flipped")
         for jb in range(NODE_BLOCKS):
@@ -154,11 +160,11 @@ def tile_spconvlayer_b_kernel(tc, x, adj_t, weight, bias, base, offs, out):
             relu_u = work.tile([P, N], F32, name="relu_u", bufs=3)
             nodes_first = cb >= CHANNELS_FIRST_BLOCKS
             if nodes_first:
-                averaged = average_nodes_first(projected)
+                averaged = average_nodes_first(projected[cb])
             else:
-                average_channels_first(projected, relu_u)
-            if cb + 1 < CHANNEL_BLOCKS:
-                projected = project(cb + 1)
+                average_channels_first(projected[cb], relu_u)
+            while len(halves_done) < min(HALVES * cb + 5, HALVES * CHANNEL_BLOCKS):
+                project_half()
             if nodes_first:
                 flip(averaged, relu_u)
 

@@ -163,10 +163,12 @@ def tile_spconvlayer_b_kernel(tc, x, adj_t, weight, bias, base, offs, out):
                 averaged = average_nodes_first(projected[cb])
             else:
                 average_channels_first(projected[cb], relu_u)
-            while len(halves_done) < min(HALVES * cb + 5, HALVES * CHANNEL_BLOCKS):
+            while len(halves_done) < min(HALVES * cb + 4, HALVES * CHANNEL_BLOCKS):
                 project_half()
             if nodes_first:
                 flip(averaged, relu_u)
+            if len(halves_done) < HALVES * CHANNEL_BLOCKS:
+                project_half()
 
             nc.vector.tensor_tensor(
                 windows[cb][:].indirect(offsets[:]), relu_u[:], bias_wide[cb][:], ALU.add

@@ -44,8 +44,9 @@ def tile_spconvlayer_b_kernel(tc, x, adj_t, weight, bias, base, offs, out):
             cols = slice(half * BANK, (half + 1) * BANK)
             nc.sync.dma_start(neighbours[half][:], adj_t[:, cols].rearrange("(kb p) j -> p kb j", p=P))
 
-        bias_cols = held.tile([P, CHANNEL_BLOCKS], F32, name="bias_cols")
-        nc.sync.dma_start(bias_cols[:], bias.rearrange("(b p) o -> p (b o)", p=P))
+        bias_rows = held.tile([P, P], F32, name="bias_rows")
+        nc.gpsimd.memset(bias_rows[:], 0.0)
+        nc.sync.dma_start(bias_rows[0:CHANNEL_BLOCKS, :], bias.rearrange("(b p) o -> b (p o)", p=P))
 
         windows = [held.tile([P, S], F32, name=f"window{cb}") for cb in range(CHANNEL_BLOCKS)]
         nc.sync.dma_start(weights[:, :, P : 2 * P], weight_amc[:, :, P : 2 * P])
@@ -148,6 +149,10 @@ def tile_spconvlayer_b_kernel(tc, x, adj_t, weight, bias, base, offs, out):
         inv_degree_row = held.tile([P, N], F32, name="inv_degree_row")
         flip(inv_degree_spread, inv_degree_row)
 
+        bias_flipped = psum.tile([P, P], F32, name="bias_flipped", tag="flipped")
+        nc.tensor.transpose(bias_flipped[:], bias_rows[:], identity_f32[:])
+        bias_cols = held.tile([P, CHANNEL_BLOCKS], F32, name="bias_cols")
+        nc.vector.tensor_copy(bias_cols[:], bias_flipped[:, 0:CHANNEL_BLOCKS])
         bias_wide = [held.tile([P, N], F32, name=f"bias_wide{cb}") for cb in range(CHANNEL_BLOCKS)]
         for cb in range(CHANNEL_BLOCKS):
             repeated = bias_cols[:, cb : cb + 1].to_broadcast([P, N])

@@ -30,6 +30,8 @@ def tile_spconvlayer_b_kernel(tc, x, adj_t, weight, bias, base, offs, out):
         offsets = held.tile([P, N // 16], U16, name="offsets")
         nc.sync.dma_start(offsets[:], offs)
 
+        bias_rows = held.tile([P, P], F32, name="bias_rows")
+        nc.gpsimd.memset(bias_rows[:], 0.0)
         weights = held.tile([P, M, C], BF16, name="weights")
         weight_amc = weight.rearrange("m a c -> a m c")
         features = held.tile([P, M, N], BF16, name="features")
@@ -38,15 +40,13 @@ def tile_spconvlayer_b_kernel(tc, x, adj_t, weight, bias, base, offs, out):
         for quarter in range(4):
             cols = slice(quarter * (N // 4), (quarter + 1) * (N // 4))
             nc.sync.dma_start(features[:, :, cols], x_amk[:, :, cols])
+            if quarter == 0:
+                nc.sync.dma_start(bias_rows[0:CHANNEL_BLOCKS, :], bias.rearrange("(b p) o -> b (p o)", p=P))
 
         neighbours = [held.tile([P, NODE_BLOCKS, BANK], BF16, name=f"neighbours{half}") for half in range(HALVES)]
         for half in range(HALVES):
             cols = slice(half * BANK, (half + 1) * BANK)
             nc.sync.dma_start(neighbours[half][:], adj_t[:, cols].rearrange("(kb p) j -> p kb j", p=P))
-
-        bias_rows = held.tile([P, P], F32, name="bias_rows")
-        nc.gpsimd.memset(bias_rows[:], 0.0)
-        nc.sync.dma_start(bias_rows[0:CHANNEL_BLOCKS, :], bias.rearrange("(b p) o -> b (p o)", p=P))
 
         windows = [held.tile([P, S], F32, name=f"window{cb}") for cb in range(CHANNEL_BLOCKS)]
         nc.sync.dma_start(weights[:, :, P : 2 * P], weight_amc[:, :, P : 2 * P])
@@ -61,6 +61,18 @@ def tile_spconvlayer_b_kernel(tc, x, adj_t, weight, bias, base, offs, out):
         make_identity(nc, identity_bf16[:])
         ones = held.tile([P, 1], BF16, name="ones")
         nc.vector.memset(ones[:], 1.0)
+
+        bias_flipped = psum.tile([P, P], F32, name="bias_flipped", tag="flipped")
+        nc.tensor.transpose(bias_flipped[:], bias_rows[:], identity_f32[:])
+        bias_cols = held.tile([P, CHANNEL_BLOCKS], F32, name="bias_cols")
+        nc.vector.tensor_copy(bias_cols[:], bias_flipped[:, 0:CHANNEL_BLOCKS])
+        bias_wide = [held.tile([P, N], F32, name=f"bias_wide{cb}") for cb in range(CHANNEL_BLOCKS)]
+        for cb in range(CHANNEL_BLOCKS):
+            repeated = bias_cols[:, cb : cb + 1].to_broadcast([P, N])
+            if cb % 3 == 0:
+                nc.scalar.copy(bias_wide[cb][:], repeated)
+            else:
+                nc.vector.tensor_copy(bias_wide[cb][:], repeated)
 
         def received(kb, jb):
             first = (jb % BLOCKS_PER_BANK) * P
@@ -148,18 +160,6 @@ def tile_spconvlayer_b_kernel(tc, x, adj_t, weight, bias, base, offs, out):
         nc.vector.tensor_copy(inv_degree_spread[:], inv_degree[:].unsqueeze(2).to_broadcast([P, NODE_BLOCKS, P]))
         inv_degree_row = held.tile([P, N], F32, name="inv_degree_row")
         flip(inv_degree_spread, inv_degree_row)
-
-        bias_flipped = psum.tile([P, P], F32, name="bias_flipped", tag="flipped")
-        nc.tensor.transpose(bias_flipped[:], bias_rows[:], identity_f32[:])
-        bias_cols = held.tile([P, CHANNEL_BLOCKS], F32, name="bias_cols")
-        nc.vector.tensor_copy(bias_cols[:], bias_flipped[:, 0:CHANNEL_BLOCKS])
-        bias_wide = [held.tile([P, N], F32, name=f"bias_wide{cb}") for cb in range(CHANNEL_BLOCKS)]
-        for cb in range(CHANNEL_BLOCKS):
-            repeated = bias_cols[:, cb : cb + 1].to_broadcast([P, N])
-            if cb % 3 == 0:
-                nc.scalar.copy(bias_wide[cb][:], repeated)
-            else:
-                nc.vector.tensor_copy(bias_wide[cb][:], repeated)
 
         for cb in range(CHANNEL_BLOCKS):
             relu_u = work.tile([P, N], F32, name="relu_u", bufs=3)

@@ -43,10 +43,12 @@ def tile_spconvlayer_b_kernel(tc, x, adj_t, weight, bias, base, offs, out):
             if quarter == 0:
                 nc.sync.dma_start(bias_rows[0:CHANNEL_BLOCKS, :], bias.rearrange("(b p) o -> b (p o)", p=P))
 
-        neighbours = [held.tile([P, NODE_BLOCKS, BANK], BF16, name=f"neighbours{half}") for half in range(HALVES)]
-        for half in range(HALVES):
-            cols = slice(half * BANK, (half + 1) * BANK)
-            nc.sync.dma_start(neighbours[half][:], adj_t[:, cols].rearrange("(kb p) j -> p kb j", p=P))
+        neighbours = held.tile([P, NODE_BLOCKS, N], BF16, name="neighbours")
+        for kb in range(0, NODE_BLOCKS, 2):
+            nc.sync.dma_start(
+                neighbours[:, kb : kb + 2, :],
+                adj_t[kb * P : (kb + 2) * P, :].rearrange("(kb p) j -> p kb j", p=P),
+            )
 
         windows = [held.tile([P, S], F32, name=f"window{cb}") for cb in range(CHANNEL_BLOCKS)]
         nc.sync.dma_start(weights[:, :, P : 2 * P], weight_amc[:, :, P : 2 * P])
@@ -75,8 +77,7 @@ def tile_spconvlayer_b_kernel(tc, x, adj_t, weight, bias, base, offs, out):
                 nc.vector.tensor_copy(bias_wide[cb][:], repeated)
 
         def received(kb, jb):
-            first = (jb % BLOCKS_PER_BANK) * P
-            return neighbours[jb // BLOCKS_PER_BANK][:, kb, first : first + P]
+            return neighbours[:, kb, jb * P : (jb + 1) * P]
 
         projected = []
 
@@ -132,7 +133,7 @@ def tile_spconvlayer_b_kernel(tc, x, adj_t, weight, bias, base, offs, out):
                 u_sums = psum.tile([P, BANK], F32, name="u_sums", bufs=4)
                 for kb in range(NODE_BLOCKS):
                     nc.tensor.matmul(
-                        u_sums[:], projected[:, kb, :], neighbours[half][:, kb, :],
+                        u_sums[:], projected[:, kb, :], neighbours[:, kb, cols],
                         start=(kb == 0), stop=(kb == NODE_BLOCKS - 1),
                     )
                 nc.vector.scalar_tensor_tensor(
@@ -142,15 +143,16 @@ def tile_spconvlayer_b_kernel(tc, x, adj_t, weight, bias, base, offs, out):
         for bank in range(HALVES):
             project_half()
 
-        degree_sums = psum.tile([P, NODE_BLOCKS], F32, name="degree_sums", tag="flipped")
-        for jb in range(NODE_BLOCKS):
-            for kb in range(NODE_BLOCKS):
+        degree_parts = psum.tile([P, NODE_BLOCKS, NODE_BLOCKS], F32, name="degree_parts", tag="flipped")
+        for kb in range(NODE_BLOCKS):
+            for jb in range(NODE_BLOCKS):
                 nc.tensor.matmul(
-                    degree_sums[:, jb : jb + 1], received(kb, jb), ones[:],
-                    start=(kb == 0), stop=(kb == NODE_BLOCKS - 1),
+                    degree_parts[:, jb, kb : kb + 1], received(kb, jb), ones[:], start=True, stop=True
                 )
-            nc.vector.tensor_tensor(received(jb, jb), received(jb, jb), identity_bf16[:], ALU.add)
+            nc.vector.tensor_tensor(received(kb, kb), received(kb, kb), identity_bf16[:], ALU.add)
 
+        degree_sums = held.tile([P, NODE_BLOCKS], F32, name="degree_sums")
+        nc.vector.tensor_reduce(degree_sums[:], degree_parts[:], mybir.AxisListType.X, ALU.add)
         degree = held.tile([P, NODE_BLOCKS], F32, name="degree")
         nc.vector.tensor_scalar_add(degree[:], degree_sums[:], 1.0)
         inv_degree = held.tile([P, NODE_BLOCKS], F32, name="inv_degree")

import concourse.mybir as mybir
from concourse.masks import make_identity

BF16, F32, U16 = mybir.dt.bfloat16, mybir.dt.float32, mybir.dt.uint16
ALU = mybir.AluOpType
RELU = mybir.ActivationFunctionType.Relu

P = 128
M = 4
N = 1024
C = 1024
S = 2048
BANK = 512
NODE_BLOCKS = N // P
CHANNEL_BLOCKS = C // P
HALVES = N // BANK
BLOCKS_PER_BANK = BANK // P
CHANNELS_FIRST_BLOCKS = 4

FLOPS = 2 * M * P * C * N + 2 * C * N * N


def tile_spconvlayer_b_kernel(tc, x, adj_t, weight, bias, base, offs, out):
    nc = tc.nc
    with (
        tc.tile_pool(name="held", bufs=1) as held,
        tc.tile_pool(name="work", bufs=2) as work,
        tc.psum_pool(name="psum", bufs=2) as psum,
    ):
        offsets = held.tile([P, N // 16], U16, name="offsets")
        nc.sync.dma_start(offsets[:], offs)

        bias_rows = held.tile([P, P], F32, name="bias_rows")
        nc.gpsimd.memset(bias_rows[:], 0.0)
        weights = held.tile([P, M, C], BF16, name="weights")
        weight_amc = weight.rearrange("m a c -> a m c")
        features = held.tile([P, M, N], BF16, name="features")
        x_amk = x.rearrange("m a k -> a m k")
        nc.sync.dma_start(weights[:, :, 0:P], weight_amc[:, :, 0:P])
        for quarter in range(4):
            cols = slice(quarter * (N // 4), (quarter + 1) * (N // 4))
            nc.sync.dma_start(features[:, :, cols], x_amk[:, :, cols])
            if quarter == 0:
                nc.sync.dma_start(bias_rows[0:CHANNEL_BLOCKS, :], bias.rearrange("(b p) o -> b (p o)", p=P))

        neighbours = held.tile([P, NODE_BLOCKS, N], BF16, name="neighbours")
        for kb in range(0, NODE_BLOCKS, 2):
            nc.sync.dma_start(
                neighbours[:, kb : kb + 2, :],
                adj_t[kb * P : (kb + 2) * P, :].rearrange("(kb p) j -> p kb j", p=P),
            )

        windows = [held.tile([P, S], F32, name=f"window{cb}") for cb in range(CHANNEL_BLOCKS)]
        nc.sync.dma_start(weights[:, :, P : 2 * P], weight_amc[:, :, P : 2 * P])
        nc.sync.dma_start(windows[0][:], base[0:P, :])
        nc.sync.dma_start(weights[:, :, 2 * P : C], weight_amc[:, :, 2 * P : C])
        for cb in range(1, CHANNEL_BLOCKS):
            nc.sync.dma_start(windows[cb][:], base[cb * P : (cb + 1) * P, :])

        identity_f32 = held.tile([P, P], F32, name="identity_f32")
        make_identity(nc, identity_f32[:])
        identity_bf16 = held.tile([P, P], BF16, name="identity_bf16")
        make_identity(nc, identity_bf16[:])
        ones = held.tile([P, 1], BF16, name="ones")
        nc.vector.memset(ones[:], 1.0)

        bias_flipped = psum.tile([P, P], F32, name="bias_flipped", tag="flipped")
        nc.tensor.transpose(bias_flipped[:], bias_rows[:], identity_f32[:])
        bias_cols = held.tile([P, CHANNEL_BLOCKS], F32, name="bias_cols")
        nc.vector.tensor_copy(bias_cols[:], bias_flipped[:, 0:CHANNEL_BLOCKS])
        bias_wide = [held.tile([P, N], F32, name=f"bias_wide{cb}") for cb in range(CHANNEL_BLOCKS)]
        for cb in range(CHANNEL_BLOCKS):
            repeated = bias_cols[:, cb : cb + 1].to_broadcast([P, N])
            if cb % 3 == 0:
                nc.scalar.copy(bias_wide[cb][:], repeated)
            else:
                nc.vector.tensor_copy(bias_wide[cb][:], repeated)

        def received(kb, jb):
            return neighbours[:, kb, jb * P : (jb + 1) * P]

        projected = []

        def project_half():
            cb, bank = divmod(len(halves_done), HALVES)
            halves_done.append((cb, bank))
            if bank == 0:
                projected.append(work.tile([P, NODE_BLOCKS, P], BF16, name="projected", bufs=3))
            h_sums = psum.tile([P, BLOCKS_PER_BANK, P], F32, name="h_sums")
            for i in range(BLOCKS_PER_BANK):
                kb = bank * BLOCKS_PER_BANK + i
                for m in range(M):
                    nc.tensor.matmul(
                        h_sums[:, i, :], features[:, m, kb * P : (kb + 1) * P],
                        weights[:, m, cb * P : (cb + 1) * P],
                        start=(m == 0), stop=(m == M - 1),
                    )
            nc.scalar.copy(
                projected[cb][:, bank * BLOCKS_PER_BANK : (bank + 1) * BLOCKS_PER_BANK, :], h_sums[:]
            )

        halves_done = []

        def average_nodes_first(projected):
            averaged = work.tile([P, NODE_BLOCKS, P], F32, name="averaged")
            for bank in range(HALVES):
                u_sums = psum.tile([P, BLOCKS_PER_BANK, P], F32, name="u_sums", bufs=4)
                for i in range(BLOCKS_PER_BANK):
                    jb = bank * BLOCKS_PER_BANK + i
                    for kb in range(NODE_BLOCKS):
                        nc.tensor.matmul(
                            u_sums[:, i, :], received(kb, jb), projected[:, kb, :],
                            start=(kb == 0), stop=(kb == NODE_BLOCKS - 1),
                        )
                for i in range(BLOCKS_PER_BANK):
                    jb = bank * BLOCKS_PER_BANK + i
                    nc.scalar.activation(
                        averaged[:, jb, :], u_sums[:, i, :], RELU, scale=inv_degree[:, jb : jb + 1]
                    )
            return averaged

        def flip(nodes_first, channels_first):
            for bank in range(HALVES):
                flipped = psum.tile([P, BANK], F32, name="flipped")
                for i in range(BLOCKS_PER_BANK):
                    jb = bank * BLOCKS_PER_BANK + i
                    nc.tensor.transpose(flipped[:, i * P : (i + 1) * P], nodes_first[:, jb, :], identity_f32[:])
                nc.scalar.copy(channels_first[:, bank * BANK : (bank + 1) * BANK], flipped[:])

        def average_channels_first(projected, relu_u):
            for half in range(HALVES):
                cols = slice(half * BANK, (half + 1) * BANK)
                u_sums = psum.tile([P, BANK], F32, name="u_sums", bufs=4)
                for kb in range(NODE_BLOCKS):
                    nc.tensor.matmul(
                        u_sums[:], projected[:, kb, :], neighbours[:, kb, cols],
                        start=(kb == 0), stop=(kb == NODE_BLOCKS - 1),
                    )
                nc.vector.scalar_tensor_tensor(
                    relu_u[:, cols], u_sums[:], 0.0, inv_degree_row[:, cols], ALU.max, ALU.mult
                )

        for bank in range(HALVES):
            project_half()

        degree_parts = psum.tile([P, NODE_BLOCKS, NODE_BLOCKS], F32, name="degree_parts", tag="flipped")
        for kb in range(NODE_BLOCKS):
            for jb in range(NODE_BLOCKS):
                nc.tensor.matmul(
                    degree_parts[:, jb, kb : kb + 1], received(kb, jb), ones[:], start=True, stop=True
                )
            nc.vector.tensor_tensor(received(kb, kb), received(kb, kb), identity_bf16[:], ALU.add)

        degree_sums = held.tile([P, NODE_BLOCKS], F32, name="degree_sums")
        nc.vector.tensor_reduce(degree_sums[:], degree_parts[:], mybir.AxisListType.X, ALU.add)
        degree = held.tile([P, NODE_BLOCKS], F32, name="degree")
        nc.vector.tensor_scalar_add(degree[:], degree_sums[:], 1.0)
        inv_degree = held.tile([P, NODE_BLOCKS], F32, name="inv_degree")
        nc.vector.reciprocal(inv_degree[:], degree[:])

        inv_degree_spread = held.tile([P, NODE_BLOCKS, P], F32, name="inv_degree_spread")
        nc.vector.tensor_copy(inv_degree_spread[:], inv_degree[:].unsqueeze(2).to_broadcast([P, NODE_BLOCKS, P]))
        inv_degree_row = held.tile([P, N], F32, name="inv_degree_row")
        flip(inv_degree_spread, inv_degree_row)

        for cb in range(CHANNEL_BLOCKS):
            relu_u = work.tile([P, N], F32, name="relu_u", bufs=3)
            nodes_first = cb >= CHANNELS_FIRST_BLOCKS
            if nodes_first:
                averaged = average_nodes_first(projected[cb])
            else:
                average_channels_first(projected[cb], relu_u)
            while len(halves_done) < min(HALVES * cb + 4, HALVES * CHANNEL_BLOCKS):
                project_half()
            if nodes_first:
                flip(averaged, relu_u)
            if len(halves_done) < HALVES * CHANNEL_BLOCKS:
                project_half()

            nc.vector.tensor_tensor(
                windows[cb][:].indirect(offsets[:]), relu_u[:], bias_wide[cb][:], ALU.add
            )
            nc.sync.dma_start(out[cb * P : (cb + 1) * P, :], windows[cb][:])
